import numpy as np
import ml_dtypes


def mxq(x, axis, fmt="e4m3"):
    dtype, down = {"e4m3": (ml_dtypes.float8_e4m3fn, 7), "e5m2": (ml_dtypes.float8_e5m2, 14)}[fmt]
    v = np.moveaxis(np.asarray(x, np.float32).astype(ml_dtypes.bfloat16).astype(np.float64), axis, -1)
    blocks = v.reshape(v.shape[:-1] + (-1, 32))
    amax = np.abs(blocks).max(-1, keepdims=True)
    byte = np.maximum(np.where(amax > 0, np.frexp(amax)[1] - 1 + 127, 0) - down, 1)
    scale = np.exp2(byte - 127.0)
    codes = (blocks / scale).astype(np.float32).astype(dtype).astype(np.float64)
    return np.moveaxis((codes * scale).reshape(v.shape), -1, axis)


WIDE = False


def mx_kscale(k):
    if not WIDE:
        return np.ones(k)
    levels = np.array([10, -10, 5, -5, 0])
    a = np.random.permutation(np.resize(levels, k // 512 * 4)).reshape(k // 512, 4)
    idx = np.arange(k)
    return np.exp2(a[idx // 512, idx % 128 // 32])


BF16 = ml_dtypes.bfloat16


def bf(x):
    return np.asarray(x, np.float32).astype(BF16)


def f64(x):
    return np.asarray(x).astype(np.float64)


E2M1 = np.array([0.0, 0.5, 1.0, 1.5, 2.0, 3.0, 4.0, 6.0, -0.0, -0.5, -1.0, -1.5, -2.0, -3.0, -4.0, -6.0])


def pack_weight(w, fmt):
    k, n = w.shape
    w = f64(bf(w)).reshape(k // 32, 32, n)
    amax = np.abs(w).max(1)
    if fmt == "e4m3":
        byte = np.frexp(amax)[1] - 1 + 127 - 7
    else:
        mant, ex = np.frexp(amax / 6.0)
        byte = np.where(mant > 0.5, ex, ex - 1) + 127
    byte = np.clip(np.where(amax > 0, byte, 1), 1, 254)
    scaled = (w * np.exp2(127.0 - byte)[:, None, :]).reshape(k, n).astype(np.float32)
    by_word = np.ascontiguousarray(scaled.reshape(k // 512, 128, 4, n).transpose(0, 1, 3, 2))
    if fmt == "e4m3":
        words = by_word.astype(ml_dtypes.float8_e4m3fn).view(np.uint8)
    else:
        c = by_word.astype(ml_dtypes.float4_e2m1fn).view(np.uint8) & 0xF
        words = c[..., 0::2] | (c[..., 1::2] << 4)
    return np.ascontiguousarray(words), np.ascontiguousarray(byte.astype(np.uint8).reshape(k // 512, 16, n))


def unpack_weight(words, scales, fmt):
    g, p, n, _ = words.shape
    if fmt == "e4m3":
        vals = np.ascontiguousarray(words).view(ml_dtypes.float8_e4m3fn).astype(np.float64)
    else:
        nib = np.empty((g, p, n, 4), np.uint8)
        nib[..., 0::2] = words & 0xF
        nib[..., 1::2] = words >> 4
        vals = E2M1[nib]
    vals = vals * np.repeat(np.exp2(scales.astype(np.float64) - 127.0), 8, axis=1)[..., None]
    return vals.transpose(0, 1, 3, 2).reshape(g * 512, n)


N, B, T, C, R, O, NC, H, W = 31, 128, 4, 256, 4, 512, 512, 16, 4
K = C * R
LEAKY_SLOPE = 0.01


def setup_inputs():
    s = mx_kscale(K)
    pooled = bf((0.65 + 0.3 * np.random.standard_normal((N, B, K))) * s)
    p = bf(0.65 + 0.5 * np.random.standard_normal((N, B, T, C)))
    stack = (4.0 / np.sqrt(K) * np.random.standard_normal((N, K, C)) - 4.0 / K) / s[None, :, None]
    words, scales = pack_weight(stack.reshape(-1, C), "e4m3")
    return {"pooled": pooled,
            "p": p,
            "Wout_words": words,
            "Wout_scales": scales}


def reference(pooled, p, Wout_words, Wout_scales):
    y = mxq(f64(pooled), 2, "e4m3") @ unpack_weight(Wout_words, Wout_scales, "e4m3").reshape(N, K, C)
    y = np.where(y >= 0, y, LEAKY_SLOPE * y)
    return np.max(f64(p) + y[:, :, None, :], axis=2)

@@ -1,0 +1,203 @@
+from contextlib import ExitStack
+
+import concourse.mybir as mybir
+from concourse.masks import make_identity
+
+BF16 = mybir.dt.bfloat16
+F32 = mybir.dt.float32
+I32 = mybir.dt.int32
+U32 = mybir.dt.uint32
+U8 = mybir.dt.uint8
+FP8X4 = mybir.dt.float8_e4m3fn_x4
+MAX = mybir.AluOpType.max
+ADD = mybir.AluOpType.add
+
+P = 128
+N_BINS = 31
+B = 128
+FRAMES = 4
+C = 256
+K = 1024
+LEAKY_SLOPE = 0.01
+
+PACK = 4
+K_PASS = P * PACK
+PASSES = K // K_PASS
+PAIRS = PACK // 2
+N_GROUPS = N_BINS * PASSES
+
+UNIT_BINS = 2
+N_UNITS = (N_BINS + UNIT_BINS - 1) // UNIT_BINS
+
+PLANE_STARTS = 4
+PLANE_SLOTS = (N_GROUPS + PLANE_STARTS - 1) // PLANE_STARTS
+SCALE_ROWS = 16
+QUADRANT = 32
+ROWS_PER_QUADRANT = SCALE_ROWS * QUADRANT // P
+
+LOAD_AHEAD = 3
+LOAD_BUFS = LOAD_AHEAD + 3
+RESULT_BUFS = LOAD_AHEAD + 2
+
+FLOPS = 2 * N_BINS * B * K * C
+
+
+def tile_gmpahead_pa_e_kernel(tc, pooled, p, Wout_words, Wout_scales, out):
+    nc = tc.nc
+
+    with ExitStack() as ctx:
+        const = ctx.enter_context(tc.tile_pool(name="const", bufs=1))
+        loads = ctx.enter_context(tc.tile_pool(name="loads", bufs=LOAD_BUFS))
+        work = ctx.enter_context(tc.tile_pool(name="work", bufs=2))
+        results = ctx.enter_context(tc.tile_pool(name="results", bufs=RESULT_BUFS))
+        psum_t = ctx.enter_context(tc.psum_pool(name="psum_t", bufs=2 * UNIT_BINS))
+        psum_y = ctx.enter_context(tc.psum_pool(name="psum_y", bufs=3))
+
+        planes = const.tile([P, PLANE_SLOTS, C], U8, align_bytes=64)
+        nc.vector.memset(planes[:].rearrange("p s c -> p (s c)").bitcast(I32), 0)
+
+        identity = const.tile([P, P], F32)
+        make_identity(nc, identity[:])
+
+        pooled_of = {}
+        weights_of = {}
+        frames_of = {}
+        codes_of = {}
+        code_scales_of = {}
+
+        def bins_of(u):
+            first = u * UNIT_BINS
+            return first, min(UNIT_BINS, N_BINS - first)
+
+        def load_scale_planes(start):
+            first = start * PLANE_SLOTS
+            count = min(PLANE_SLOTS, N_GROUPS - first)
+            rows = Wout_scales[first : first + count].rearrange(
+                "s (q r) c -> r q s c", r=ROWS_PER_QUADRANT
+            )
+            for r in range(ROWS_PER_QUADRANT):
+                nc.sync.dma_start(
+                    out=planes[ROWS_PER_QUADRANT * start + r : P : QUADRANT, 0:count, :].bitcast(I32),
+                    in_=rows[r].bitcast(I32),
+                )
+
+        def load_pooled(u):
+            if u >= N_UNITS:
+                return
+            first, bins = bins_of(u)
+            pooled_sb = loads.tile([P, UNIT_BINS, K], BF16)
+            nc.sync.dma_start(
+                out=pooled_sb[:, 0:bins, :],
+                in_=pooled[first : first + bins].rearrange("n b k -> b n k"),
+            )
+            pooled_of[u] = pooled_sb
+
+        def load_weights_and_frames(u):
+            if u >= N_UNITS:
+                return
+            first, bins = bins_of(u)
+            groups = bins * PASSES
+            if (first * PASSES) % PLANE_SLOTS == 0:
+                load_scale_planes(first * PASSES // PLANE_SLOTS)
+            w_sb = loads.tile([P, UNIT_BINS * PASSES, C], U32, align_bytes=64)
+            nc.sync.dma_start(
+                out=w_sb[:, 0:groups, :].bitcast(I32),
+                in_=Wout_words[first * PASSES : first * PASSES + groups]
+                .rearrange("g r c t -> r g (c t)")
+                .bitcast(I32),
+            )
+            weights_of[u] = w_sb
+            p_sb = loads.tile([P, UNIT_BINS, FRAMES, C], BF16)
+            nc.sync.dma_start(
+                out=p_sb[:, 0:bins],
+                in_=p[first : first + bins].rearrange("n b t c -> b n t c"),
+            )
+            frames_of[u] = p_sb
+
+        def transpose_and_quantise(u):
+            if u >= N_UNITS:
+                return
+            first, bins = bins_of(u)
+            words = pooled_of[u][:].rearrange("b n k -> b (n k)").bitcast(F32)
+            words_per_pass = K_PASS // 2
+            grouped = work.tile([P, UNIT_BINS * PASSES * B * PACK], BF16, align_bytes=64)
+            grouped_words = grouped[:].bitcast(F32).rearrange(
+                "r (n g b u) -> r n g b u", n=UNIT_BINS, g=PASSES, b=B
+            )
+            for i in range(bins):
+                xt = psum_t.tile([P, PASSES, PAIRS, B], F32)
+                for g in range(PASSES):
+                    begin = (i * PASSES + g) * words_per_pass
+                    for u2 in range(PAIRS):
+                        nc.tensor.transpose(
+                            xt[:, g, u2, :],
+                            words[:, begin + u2 : begin + words_per_pass : PAIRS],
+                            identity[:],
+                        )
+                nc.scalar.copy(out=grouped_words[:, i], in_=xt[:].rearrange("r g u b -> r g b u"))
+            columns = bins * PASSES * B
+            codes = work.tile([P, UNIT_BINS * PASSES * B], U32, align_bytes=64)
+            code_scales = work.tile([P, UNIT_BINS * PASSES * B], U8, align_bytes=64)
+            nc.vector.quantize_mx(
+                out=codes[:, 0:columns].bitcast(FP8X4),
+                scales=code_scales[:, 0:columns],
+                in_=grouped[:, 0 : columns * PACK],
+            )
+            codes_of[u] = codes
+            code_scales_of[u] = code_scales
+
+        def multiply_and_finish(u):
+            first, bins = bins_of(u)
+            p_sb = frames_of[u]
+            y = psum_y.tile([P, UNIT_BINS, C], F32)
+            for i in range(bins):
+                for g in range(PASSES):
+                    group = (first + i) * PASSES + g
+                    plane_start = ROWS_PER_QUADRANT * (group // PLANE_SLOTS)
+                    b_cols = slice((i * PASSES + g) * B, (i * PASSES + g + 1) * B)
+                    nc.tensor.matmul_mx(
+                        out=y[:, i, :],
+                        lhsT=codes_of[u][:, b_cols].bitcast(FP8X4),
+                        lhsT_scale=code_scales_of[u][:, b_cols],
+                        rhs=weights_of[u][:, i * PASSES + g, :].bitcast(FP8X4),
+                        rhs_scale=planes[plane_start:P, group % PLANE_SLOTS, :],
+                        start=(g == 0),
+                        stop=(g == PASSES - 1),
+                    )
+            sloped = work.tile([P, UNIT_BINS, C], F32)
+            nc.scalar.mul(out=sloped[:, 0:bins], in_=y[:, 0:bins], mul=LEAKY_SLOPE)
+            two_frames = work.tile([P, UNIT_BINS, FRAMES // 2, C], BF16)
+            nc.vector.tensor_tensor(
+                out=two_frames[:, 0:bins],
+                in0=p_sb[:, 0:bins, 0 : FRAMES // 2, :],
+                in1=p_sb[:, 0:bins, FRAMES // 2 : FRAMES, :],
+                op=MAX,
+            )
+            leaky = work.tile([P, UNIT_BINS, C], F32)
+            nc.vector.tensor_tensor(out=leaky[:, 0:bins], in0=y[:, 0:bins], in1=sloped[:, 0:bins], op=MAX)
+            top_frame = work.tile([P, UNIT_BINS, C], BF16)
+            nc.vector.tensor_tensor(
+                out=top_frame[:, 0:bins],
+                in0=two_frames[:, 0:bins, 0, :],
+                in1=two_frames[:, 0:bins, 1, :],
+                op=MAX,
+            )
+            feat = results.tile([P, UNIT_BINS, C], F32)
+            nc.vector.tensor_tensor(
+                out=feat[:, 0:bins], in0=leaky[:, 0:bins], in1=top_frame[:, 0:bins], op=ADD
+            )
+            nc.sync.dma_start(
+                out=out[first : first + bins].rearrange("n b c -> b n c"), in_=feat[:, 0:bins]
+            )
+
+        with tc.manual_schedule():
+            load_pooled(0)
+            for u in range(LOAD_AHEAD):
+                load_pooled(u + 1)
+                load_weights_and_frames(u)
+            transpose_and_quantise(0)
+            for u in range(N_UNITS):
+                load_pooled(u + LOAD_AHEAD + 1)
+                load_weights_and_frames(u + LOAD_AHEAD)
+                transpose_and_quantise(u + 1)
+                multiply_and_finish(u)

@@ -29,11 +29,11 @@ N_GROUPS = N_BINS * PASSES
 UNIT_BINS = 2
 N_UNITS = (N_BINS + UNIT_BINS - 1) // UNIT_BINS
 
-PLANE_STARTS = 4
-PLANE_SLOTS = (N_GROUPS + PLANE_STARTS - 1) // PLANE_STARTS
 SCALE_ROWS = 16
 QUADRANT = 32
 ROWS_PER_QUADRANT = SCALE_ROWS * QUADRANT // P
+PLANE_SET = 16
+N_PLANE_SETS = (N_GROUPS + PLANE_SET - 1) // PLANE_SET
 
 LOAD_AHEAD = 3
 LOAD_BUFS = LOAD_AHEAD + 3
@@ -53,8 +53,11 @@ def tile_gmpahead_pa_e_kernel(tc, pooled, p, Wout_words, Wout_scales, out):
         psum_t = ctx.enter_context(tc.psum_pool(name="psum_t", bufs=2 * UNIT_BINS))
         psum_y = ctx.enter_context(tc.psum_pool(name="psum_y", bufs=3))
 
-        planes = const.tile([P, PLANE_SLOTS, C], U8, align_bytes=64)
-        nc.vector.memset(planes[:].rearrange("p s c -> p (s c)").bitcast(I32), 0)
+        plane_sets = []
+        for s in range(N_PLANE_SETS):
+            planes = const.tile([P, PLANE_SET, C], U8, align_bytes=64, name="planes%d" % s)
+            nc.vector.memset(planes[:].rearrange("p s c -> p (s c)").bitcast(I32), 0)
+            plane_sets.append(planes)
 
         identity = const.tile([P, P], F32)
         make_identity(nc, identity[:])
@@ -69,15 +72,15 @@ def tile_gmpahead_pa_e_kernel(tc, pooled, p, Wout_words, Wout_scales, out):
             first = u * UNIT_BINS
             return first, min(UNIT_BINS, N_BINS - first)
 
-        def load_scale_planes(start):
-            first = start * PLANE_SLOTS
-            count = min(PLANE_SLOTS, N_GROUPS - first)
+        def load_scale_planes(s):
+            first = s * PLANE_SET
+            count = min(PLANE_SET, N_GROUPS - first)
             rows = Wout_scales[first : first + count].rearrange(
-                "s (q r) c -> r q s c", r=ROWS_PER_QUADRANT
+                "g (q r) c -> r q g c", r=ROWS_PER_QUADRANT
             )
             for r in range(ROWS_PER_QUADRANT):
                 nc.sync.dma_start(
-                    out=planes[ROWS_PER_QUADRANT * start + r : P : QUADRANT, 0:count, :].bitcast(I32),
+                    out=plane_sets[s][r:P:QUADRANT, 0:count, :].bitcast(I32),
                     in_=rows[r].bitcast(I32),
                 )
 
@@ -97,8 +100,8 @@ def tile_gmpahead_pa_e_kernel(tc, pooled, p, Wout_words, Wout_scales, out):
                 return
             first, bins = bins_of(u)
             groups = bins * PASSES
-            if (first * PASSES) % PLANE_SLOTS == 0:
-                load_scale_planes(first * PASSES // PLANE_SLOTS)
+            if (first * PASSES) % PLANE_SET == 0:
+                load_scale_planes(first * PASSES // PLANE_SET)
             w_sb = loads.tile([P, UNIT_BINS * PASSES, C], U32, align_bytes=64)
             nc.sync.dma_start(
                 out=w_sb[:, 0:groups, :].bitcast(I32),
@@ -153,14 +156,13 @@ def tile_gmpahead_pa_e_kernel(tc, pooled, p, Wout_words, Wout_scales, out):
             for i in range(bins):
                 for g in range(PASSES):
                     group = (first + i) * PASSES + g
-                    plane_start = ROWS_PER_QUADRANT * (group // PLANE_SLOTS)
                     b_cols = slice((i * PASSES + g) * B, (i * PASSES + g + 1) * B)
                     nc.tensor.matmul_mx(
                         out=y[:, i, :],
                         lhsT=codes_of[u][:, b_cols].bitcast(FP8X4),
                         lhsT_scale=code_scales_of[u][:, b_cols],
                         rhs=weights_of[u][:, i * PASSES + g, :].bitcast(FP8X4),
-                        rhs_scale=planes[plane_start:P, group % PLANE_SLOTS, :],
+                        rhs_scale=plane_sets[group // PLANE_SET][:, group % PLANE_SET, :],
                         start=(g == 0),
                         stop=(g == PASSES - 1),
                     )

@@ -34,6 +34,8 @@ QUADRANT = 32
 ROWS_PER_QUADRANT = SCALE_ROWS * QUADRANT // P
 PLANE_SET = 16
 N_PLANE_SETS = (N_GROUPS + PLANE_SET - 1) // PLANE_SET
+UNITS_PER_SET = PLANE_SET // (UNIT_BINS * PASSES)
+ROWS_PER_STAGE = SCALE_ROWS // UNITS_PER_SET
 
 LOAD_AHEAD = 3
 LOAD_BUFS = LOAD_AHEAD + 3
@@ -72,16 +74,25 @@ def tile_gmpahead_pa_e_kernel(tc, pooled, p, Wout_words, Wout_scales, out):
             first = u * UNIT_BINS
             return first, min(UNIT_BINS, N_BINS - first)
 
-        def load_scale_planes(s):
-            first = s * PLANE_SET
-            count = min(PLANE_SET, N_GROUPS - first)
-            rows = Wout_scales[first : first + count].rearrange(
-                "g (q r) c -> r q g c", r=ROWS_PER_QUADRANT
-            )
+        def first_group_of_set(s):
+            return min(s * PLANE_SET, N_GROUPS - PLANE_SET)
+
+        def load_first_plane_set():
+            rows = Wout_scales[0:PLANE_SET].rearrange("g (q r) c -> r q g c", r=ROWS_PER_QUADRANT)
             for r in range(ROWS_PER_QUADRANT):
                 nc.sync.dma_start(
-                    out=plane_sets[s][r:P:QUADRANT, 0:count, :].bitcast(I32),
-                    in_=rows[r].bitcast(I32),
+                    out=plane_sets[0][r:P:QUADRANT, :, :].bitcast(I32), in_=rows[r].bitcast(I32)
+                )
+
+        def load_scale_rows(s, q_rows):
+            first = first_group_of_set(s)
+            for q in q_rows:
+                partition = QUADRANT * (q // ROWS_PER_QUADRANT) + q % ROWS_PER_QUADRANT
+                nc.sync.dma_start(
+                    out=plane_sets[s][partition : partition + 1, :, :].bitcast(I32),
+                    in_=Wout_scales[first : first + PLANE_SET, q : q + 1, :]
+                    .rearrange("g o c -> o g c")
+                    .bitcast(I32),
                 )
 
         def load_pooled(u):
@@ -100,8 +111,6 @@ def tile_gmpahead_pa_e_kernel(tc, pooled, p, Wout_words, Wout_scales, out):
                 return
             first, bins = bins_of(u)
             groups = bins * PASSES
-            if (first * PASSES) % PLANE_SET == 0:
-                load_scale_planes(first * PASSES // PLANE_SET)
             w_sb = loads.tile([P, UNIT_BINS * PASSES, C], U32, align_bytes=64)
             nc.sync.dma_start(
                 out=w_sb[:, 0:groups, :].bitcast(I32),
@@ -116,6 +125,10 @@ def tile_gmpahead_pa_e_kernel(tc, pooled, p, Wout_words, Wout_scales, out):
                 in_=p[first : first + bins].rearrange("n b t c -> b n t c"),
             )
             frames_of[u] = p_sb
+            next_set = u // UNITS_PER_SET + 1
+            if next_set < N_PLANE_SETS:
+                share = u % UNITS_PER_SET
+                load_scale_rows(next_set, range(share * ROWS_PER_STAGE, (share + 1) * ROWS_PER_STAGE))
 
         def transpose_and_quantise(u):
             if u >= N_UNITS:
@@ -156,13 +169,14 @@ def tile_gmpahead_pa_e_kernel(tc, pooled, p, Wout_words, Wout_scales, out):
             for i in range(bins):
                 for g in range(PASSES):
                     group = (first + i) * PASSES + g
+                    plane_set = group // PLANE_SET
                     b_cols = slice((i * PASSES + g) * B, (i * PASSES + g + 1) * B)
                     nc.tensor.matmul_mx(
                         out=y[:, i, :],
                         lhsT=codes_of[u][:, b_cols].bitcast(FP8X4),
                         lhsT_scale=code_scales_of[u][:, b_cols],
                         rhs=weights_of[u][:, i * PASSES + g, :].bitcast(FP8X4),
-                        rhs_scale=plane_sets[group // PLANE_SET][:, group % PLANE_SET, :],
+                        rhs_scale=plane_sets[plane_set][:, group - first_group_of_set(plane_set), :],
                         start=(g == 0),
                         stop=(g == PASSES - 1),
                     )
@@ -194,7 +208,10 @@ def tile_gmpahead_pa_e_kernel(tc, pooled, p, Wout_words, Wout_scales, out):
 
         with tc.manual_schedule():
             load_pooled(0)
-            for u in range(LOAD_AHEAD):
+            load_pooled(1)
+            load_first_plane_set()
+            load_weights_and_frames(0)
+            for u in range(1, LOAD_AHEAD):
                 load_pooled(u + 1)
                 load_weights_and_frames(u)
             transpose_and_quantise(0)

@@ -34,12 +34,9 @@ QUADRANT = 32
 ROWS_PER_QUADRANT = SCALE_ROWS * QUADRANT // P
 PLANE_SET = 16
 N_PLANE_SETS = (N_GROUPS + PLANE_SET - 1) // PLANE_SET
-UNITS_PER_SET = PLANE_SET // (UNIT_BINS * PASSES)
-ROWS_PER_STAGE = SCALE_ROWS // UNITS_PER_SET
 
 LOAD_AHEAD = 3
 LOAD_BUFS = LOAD_AHEAD + 3
-RESULT_BUFS = LOAD_AHEAD + 2
 
 FLOPS = 2 * N_BINS * B * K * C
 
@@ -51,8 +48,8 @@ def tile_gmpahead_pa_e_kernel(tc, pooled, p, Wout_words, Wout_scales, out):
         const = ctx.enter_context(tc.tile_pool(name="const", bufs=1))
         loads = ctx.enter_context(tc.tile_pool(name="loads", bufs=LOAD_BUFS))
         work = ctx.enter_context(tc.tile_pool(name="work", bufs=2))
-        results = ctx.enter_context(tc.tile_pool(name="results", bufs=RESULT_BUFS))
-        psum_t = ctx.enter_context(tc.psum_pool(name="psum_t", bufs=2 * UNIT_BINS))
+        results = ctx.enter_context(tc.tile_pool(name="results", bufs=N_UNITS))
+        psum_t = ctx.enter_context(tc.psum_pool(name="psum_t", bufs=2 * PASSES))
         psum_y = ctx.enter_context(tc.psum_pool(name="psum_y", bufs=3))
 
         plane_sets = []
@@ -69,40 +66,32 @@ def tile_gmpahead_pa_e_kernel(tc, pooled, p, Wout_words, Wout_scales, out):
         frames_of = {}
         codes_of = {}
         code_scales_of = {}
+        feat_of = {}
 
         def bins_of(u):
             first = u * UNIT_BINS
             return first, min(UNIT_BINS, N_BINS - first)
 
-        def first_group_of_set(s):
-            return min(s * PLANE_SET, N_GROUPS - PLANE_SET)
-
-        def load_first_plane_set():
-            rows = Wout_scales[0:PLANE_SET].rearrange("g (q r) c -> r q g c", r=ROWS_PER_QUADRANT)
+        def load_scale_planes(s):
+            first = s * PLANE_SET
+            count = min(PLANE_SET, N_GROUPS - first)
+            rows = Wout_scales[first : first + count].rearrange(
+                "g (q r) c -> r q g c", r=ROWS_PER_QUADRANT
+            )
             for r in range(ROWS_PER_QUADRANT):
                 nc.sync.dma_start(
-                    out=plane_sets[0][r:P:QUADRANT, :, :].bitcast(I32), in_=rows[r].bitcast(I32)
-                )
-
-        def load_scale_rows(s, q_rows):
-            first = first_group_of_set(s)
-            for q in q_rows:
-                partition = QUADRANT * (q // ROWS_PER_QUADRANT) + q % ROWS_PER_QUADRANT
-                nc.sync.dma_start(
-                    out=plane_sets[s][partition : partition + 1, :, :].bitcast(I32),
-                    in_=Wout_scales[first : first + PLANE_SET, q : q + 1, :]
-                    .rearrange("g o c -> o g c")
-                    .bitcast(I32),
+                    out=plane_sets[s][r:P:QUADRANT, 0:count, :].bitcast(I32),
+                    in_=rows[r].bitcast(I32),
                 )
 
         def load_pooled(u):
             if u >= N_UNITS:
                 return
             first, bins = bins_of(u)
-            pooled_sb = loads.tile([P, UNIT_BINS, K], BF16)
+            pooled_sb = loads.tile([P, UNIT_BINS * K], BF16)
             nc.sync.dma_start(
-                out=pooled_sb[:, 0:bins, :],
-                in_=pooled[first : first + bins].rearrange("n b k -> b n k"),
+                out=pooled_sb[:, 0 : bins * K],
+                in_=pooled[first : first + bins].rearrange("n (h s) k -> (n h) (s k)", s=bins),
             )
             pooled_of[u] = pooled_sb
 
@@ -111,6 +100,8 @@ def tile_gmpahead_pa_e_kernel(tc, pooled, p, Wout_words, Wout_scales, out):
                 return
             first, bins = bins_of(u)
             groups = bins * PASSES
+            if (first * PASSES) % PLANE_SET == 0:
+                load_scale_planes(first * PASSES // PLANE_SET)
             w_sb = loads.tile([P, UNIT_BINS * PASSES, C], U32, align_bytes=64)
             nc.sync.dma_start(
                 out=w_sb[:, 0:groups, :].bitcast(I32),
@@ -125,33 +116,35 @@ def tile_gmpahead_pa_e_kernel(tc, pooled, p, Wout_words, Wout_scales, out):
                 in_=p[first : first + bins].rearrange("n b t c -> b n t c"),
             )
             frames_of[u] = p_sb
-            next_set = u // UNITS_PER_SET + 1
-            if next_set < N_PLANE_SETS:
-                share = u % UNITS_PER_SET
-                load_scale_rows(next_set, range(share * ROWS_PER_STAGE, (share + 1) * ROWS_PER_STAGE))
 
         def transpose_and_quantise(u):
             if u >= N_UNITS:
                 return
-            first, bins = bins_of(u)
-            words = pooled_of[u][:].rearrange("b n k -> b (n k)").bitcast(F32)
+            bins = bins_of(u)[1]
+            words = pooled_of[u][:].bitcast(F32)
+            words_per_row = K // 2
             words_per_pass = K_PASS // 2
+            columns = bins * PASSES * B
             grouped = work.tile([P, UNIT_BINS * PASSES * B * PACK], BF16, align_bytes=64)
-            grouped_words = grouped[:].bitcast(F32).rearrange(
-                "r (n g b u) -> r n g b u", n=UNIT_BINS, g=PASSES, b=B
+            grouped_words = (
+                grouped[:, 0 : columns * PACK]
+                .bitcast(F32)
+                .rearrange("r (n g h su) -> r g n h su", n=bins, g=PASSES, su=bins * PAIRS)
             )
-            for i in range(bins):
-                xt = psum_t.tile([P, PASSES, PAIRS, B], F32)
-                for g in range(PASSES):
-                    begin = (i * PASSES + g) * words_per_pass
+            for g in range(PASSES):
+                xt = psum_t.tile([P, UNIT_BINS * PAIRS, B], F32)
+                for s in range(bins):
+                    begin = s * words_per_row + g * words_per_pass
                     for u2 in range(PAIRS):
                         nc.tensor.transpose(
-                            xt[:, g, u2, :],
+                            xt[:, s * PAIRS + u2, :],
                             words[:, begin + u2 : begin + words_per_pass : PAIRS],
                             identity[:],
                         )
-                nc.scalar.copy(out=grouped_words[:, i], in_=xt[:].rearrange("r g u b -> r g b u"))
-            columns = bins * PASSES * B
+                nc.scalar.copy(
+                    out=grouped_words[:, g],
+                    in_=xt[:, 0 : bins * PAIRS, :].rearrange("r su (n h) -> r n h su", n=bins),
+                )
             codes = work.tile([P, UNIT_BINS * PASSES * B], U32, align_bytes=64)
             code_scales = work.tile([P, UNIT_BINS * PASSES * B], U8, align_bytes=64)
             nc.vector.quantize_mx(
@@ -169,14 +162,13 @@ def tile_gmpahead_pa_e_kernel(tc, pooled, p, Wout_words, Wout_scales, out):
             for i in range(bins):
                 for g in range(PASSES):
                     group = (first + i) * PASSES + g
-                    plane_set = group // PLANE_SET
                     b_cols = slice((i * PASSES + g) * B, (i * PASSES + g + 1) * B)
                     nc.tensor.matmul_mx(
                         out=y[:, i, :],
                         lhsT=codes_of[u][:, b_cols].bitcast(FP8X4),
                         lhsT_scale=code_scales_of[u][:, b_cols],
                         rhs=weights_of[u][:, i * PASSES + g, :].bitcast(FP8X4),
-                        rhs_scale=plane_sets[plane_set][:, group - first_group_of_set(plane_set), :],
+                        rhs_scale=plane_sets[group // PLANE_SET][:, group % PLANE_SET, :],
                         start=(g == 0),
                         stop=(g == PASSES - 1),
                     )
@@ -202,16 +194,17 @@ def tile_gmpahead_pa_e_kernel(tc, pooled, p, Wout_words, Wout_scales, out):
             nc.vector.tensor_tensor(
                 out=feat[:, 0:bins], in0=leaky[:, 0:bins], in1=top_frame[:, 0:bins], op=ADD
             )
+            feat_of[u] = feat
+
+        def store(u):
+            first, bins = bins_of(u)
             nc.sync.dma_start(
-                out=out[first : first + bins].rearrange("n b c -> b n c"), in_=feat[:, 0:bins]
+                out=out[first : first + bins].rearrange("n b c -> b n c"), in_=feat_of[u][:, 0:bins]
             )
 
         with tc.manual_schedule():
             load_pooled(0)
-            load_pooled(1)
-            load_first_plane_set()
-            load_weights_and_frames(0)
-            for u in range(1, LOAD_AHEAD):
+            for u in range(LOAD_AHEAD):
                 load_pooled(u + 1)
                 load_weights_and_frames(u)
             transpose_and_quantise(0)
@@ -220,3 +213,5 @@ def tile_gmpahead_pa_e_kernel(tc, pooled, p, Wout_words, Wout_scales, out):
                 load_weights_and_frames(u + LOAD_AHEAD)
                 transpose_and_quantise(u + 1)
                 multiply_and_finish(u)
+            for u in range(N_UNITS):
+                store(u)

@@ -100,8 +100,6 @@ def tile_gmpahead_pa_e_kernel(tc, pooled, p, Wout_words, Wout_scales, out):
                 return
             first, bins = bins_of(u)
             groups = bins * PASSES
-            if (first * PASSES) % PLANE_SET == 0:
-                load_scale_planes(first * PASSES // PLANE_SET)
             w_sb = loads.tile([P, UNIT_BINS * PASSES, C], U32, align_bytes=64)
             nc.sync.dma_start(
                 out=w_sb[:, 0:groups, :].bitcast(I32),
@@ -203,6 +201,8 @@ def tile_gmpahead_pa_e_kernel(tc, pooled, p, Wout_words, Wout_scales, out):
             )
 
         with tc.manual_schedule():
+            for s in range(N_PLANE_SETS):
+                load_scale_planes(s)
             load_pooled(0)
             for u in range(LOAD_AHEAD):
                 load_pooled(u + 1)

@@ -201,9 +201,9 @@ def tile_gmpahead_pa_e_kernel(tc, pooled, p, Wout_words, Wout_scales, out):
             )
 
         with tc.manual_schedule():
+            load_pooled(0)
             for s in range(N_PLANE_SETS):
                 load_scale_planes(s)
-            load_pooled(0)
             for u in range(LOAD_AHEAD):
                 load_pooled(u + 1)
                 load_weights_and_frames(u)

@@ -48,6 +48,7 @@ def tile_gmpahead_pa_e_kernel(tc, pooled, p, Wout_words, Wout_scales, out):
         const = ctx.enter_context(tc.tile_pool(name="const", bufs=1))
         loads = ctx.enter_context(tc.tile_pool(name="loads", bufs=LOAD_BUFS))
         work = ctx.enter_context(tc.tile_pool(name="work", bufs=2))
+        ordered_pool = ctx.enter_context(tc.tile_pool(name="ordered", bufs=3))
         results = ctx.enter_context(tc.tile_pool(name="results", bufs=N_UNITS))
         psum_t = ctx.enter_context(tc.psum_pool(name="psum_t", bufs=2 * PASSES))
         psum_y = ctx.enter_context(tc.psum_pool(name="psum_y", bufs=3))
@@ -62,6 +63,7 @@ def tile_gmpahead_pa_e_kernel(tc, pooled, p, Wout_words, Wout_scales, out):
         make_identity(nc, identity[:])
 
         pooled_of = {}
+        ordered_of = {}
         weights_of = {}
         frames_of = {}
         codes_of = {}
@@ -115,13 +117,25 @@ def tile_gmpahead_pa_e_kernel(tc, pooled, p, Wout_words, Wout_scales, out):
             )
             frames_of[u] = p_sb
 
+        def order_words(u):
+            if u >= N_UNITS:
+                return
+            bins = bins_of(u)[1]
+            row_passes = bins * PASSES
+            ordered = ordered_pool.tile([P, UNIT_BINS * K // 2], F32)
+            nc.scalar.copy(
+                out=ordered[:, 0 : bins * K // 2].rearrange("p (a w r) -> p a w r", a=row_passes, w=PAIRS),
+                in_=pooled_of[u][:, 0 : bins * K]
+                .bitcast(F32)
+                .rearrange("p (a r w) -> p a w r", a=row_passes, w=PAIRS),
+            )
+            ordered_of[u] = ordered
+
         def transpose_and_quantise(u):
             if u >= N_UNITS:
                 return
             bins = bins_of(u)[1]
-            words = pooled_of[u][:].bitcast(F32)
-            words_per_row = K // 2
-            words_per_pass = K_PASS // 2
+            words = ordered_of[u]
             columns = bins * PASSES * B
             grouped = work.tile([P, UNIT_BINS * PASSES * B * PACK], BF16, align_bytes=64)
             grouped_words = (
@@ -132,13 +146,9 @@ def tile_gmpahead_pa_e_kernel(tc, pooled, p, Wout_words, Wout_scales, out):
             for g in range(PASSES):
                 xt = psum_t.tile([P, UNIT_BINS * PAIRS, B], F32)
                 for s in range(bins):
-                    begin = s * words_per_row + g * words_per_pass
                     for u2 in range(PAIRS):
-                        nc.tensor.transpose(
-                            xt[:, s * PAIRS + u2, :],
-                            words[:, begin + u2 : begin + words_per_pass : PAIRS],
-                            identity[:],
-                        )
+                        begin = ((s * PASSES + g) * PAIRS + u2) * P
+                        nc.tensor.transpose(xt[:, s * PAIRS + u2, :], words[:, begin : begin + P], identity[:])
                 nc.scalar.copy(
                     out=grouped_words[:, g],
                     in_=xt[:, 0 : bins * PAIRS, :].rearrange("r su (n h) -> r n h su", n=bins),
@@ -204,14 +214,18 @@ def tile_gmpahead_pa_e_kernel(tc, pooled, p, Wout_words, Wout_scales, out):
             load_pooled(0)
             for s in range(N_PLANE_SETS):
                 load_scale_planes(s)
+            load_pooled(1)
             for u in range(LOAD_AHEAD):
-                load_pooled(u + 1)
+                load_pooled(u + 2)
                 load_weights_and_frames(u)
+            order_words(0)
+            order_words(1)
             transpose_and_quantise(0)
             for u in range(N_UNITS):
-                load_pooled(u + LOAD_AHEAD + 1)
+                load_pooled(u + LOAD_AHEAD + 2)
                 load_weights_and_frames(u + LOAD_AHEAD)
                 transpose_and_quantise(u + 1)
                 multiply_and_finish(u)
+                order_words(u + 2)
             for u in range(N_UNITS):
                 store(u)

@@ -224,8 +224,8 @@ def tile_gmpahead_pa_e_kernel(tc, pooled, p, Wout_words, Wout_scales, out):
             for u in range(N_UNITS):
                 load_pooled(u + LOAD_AHEAD + 2)
                 load_weights_and_frames(u + LOAD_AHEAD)
+                order_words(u + 2)
                 transpose_and_quantise(u + 1)
                 multiply_and_finish(u)
-                order_words(u + 2)
             for u in range(N_UNITS):
                 store(u)

@@ -35,7 +35,7 @@ ROWS_PER_QUADRANT = SCALE_ROWS * QUADRANT // P
 PLANE_SET = 16
 N_PLANE_SETS = (N_GROUPS + PLANE_SET - 1) // PLANE_SET
 
-LOAD_AHEAD = 3
+LOAD_AHEAD = 9
 LOAD_BUFS = LOAD_AHEAD + 3
 
 FLOPS = 2 * N_BINS * B * K * C

@@ -35,7 +35,7 @@ ROWS_PER_QUADRANT = SCALE_ROWS * QUADRANT // P
 PLANE_SET = 16
 N_PLANE_SETS = (N_GROUPS + PLANE_SET - 1) // PLANE_SET
 
-LOAD_AHEAD = 9
+LOAD_AHEAD = 7
 LOAD_BUFS = LOAD_AHEAD + 3
 
 FLOPS = 2 * N_BINS * B * K * C
@@ -47,11 +47,11 @@ def tile_gmpahead_pa_e_kernel(tc, pooled, p, Wout_words, Wout_scales, out):
     with ExitStack() as ctx:
         const = ctx.enter_context(tc.tile_pool(name="const", bufs=1))
         loads = ctx.enter_context(tc.tile_pool(name="loads", bufs=LOAD_BUFS))
-        work = ctx.enter_context(tc.tile_pool(name="work", bufs=2))
+        work = ctx.enter_context(tc.tile_pool(name="work", bufs=3))
         ordered_pool = ctx.enter_context(tc.tile_pool(name="ordered", bufs=3))
         results = ctx.enter_context(tc.tile_pool(name="results", bufs=N_UNITS))
         psum_t = ctx.enter_context(tc.psum_pool(name="psum_t", bufs=2 * PASSES))
-        psum_y = ctx.enter_context(tc.psum_pool(name="psum_y", bufs=3))
+        psum_y = ctx.enter_context(tc.psum_pool(name="psum_y", bufs=4))
 
         plane_sets = []
         for s in range(N_PLANE_SETS):
@@ -64,6 +64,12 @@ def tile_gmpahead_pa_e_kernel(tc, pooled, p, Wout_words, Wout_scales, out):
 
         pooled_of = {}
         ordered_of = {}
+        grouped_of = {}
+        y_of = {}
+        sloped_of = {}
+        two_frames_of = {}
+        top_frame_of = {}
+        leaky_of = {}
         weights_of = {}
         frames_of = {}
         codes_of = {}
@@ -131,7 +137,7 @@ def tile_gmpahead_pa_e_kernel(tc, pooled, p, Wout_words, Wout_scales, out):
             )
             ordered_of[u] = ordered
 
-        def transpose_and_quantise(u):
+        def transpose_words(u):
             if u >= N_UNITS:
                 return
             bins = bins_of(u)[1]
@@ -153,6 +159,13 @@ def tile_gmpahead_pa_e_kernel(tc, pooled, p, Wout_words, Wout_scales, out):
                     out=grouped_words[:, g],
                     in_=xt[:, 0 : bins * PAIRS, :].rearrange("r su (n h) -> r n h su", n=bins),
                 )
+            grouped_of[u] = grouped
+
+        def quantise(u):
+            if u >= N_UNITS:
+                return
+            columns = bins_of(u)[1] * PASSES * B
+            grouped = grouped_of[u]
             codes = work.tile([P, UNIT_BINS * PASSES * B], U32, align_bytes=64)
             code_scales = work.tile([P, UNIT_BINS * PASSES * B], U8, align_bytes=64)
             nc.vector.quantize_mx(
@@ -163,9 +176,8 @@ def tile_gmpahead_pa_e_kernel(tc, pooled, p, Wout_words, Wout_scales, out):
             codes_of[u] = codes
             code_scales_of[u] = code_scales
 
-        def multiply_and_finish(u):
+        def multiply(u):
             first, bins = bins_of(u)
-            p_sb = frames_of[u]
             y = psum_y.tile([P, UNIT_BINS, C], F32)
             for i in range(bins):
                 for g in range(PASSES):
@@ -182,6 +194,14 @@ def tile_gmpahead_pa_e_kernel(tc, pooled, p, Wout_words, Wout_scales, out):
                     )
             sloped = work.tile([P, UNIT_BINS, C], F32)
             nc.scalar.mul(out=sloped[:, 0:bins], in_=y[:, 0:bins], mul=LEAKY_SLOPE)
+            y_of[u] = y
+            sloped_of[u] = sloped
+
+        def halve_frames(u):
+            if u >= N_UNITS:
+                return
+            bins = bins_of(u)[1]
+            p_sb = frames_of[u]
             two_frames = work.tile([P, UNIT_BINS, FRAMES // 2, C], BF16)
             nc.vector.tensor_tensor(
                 out=two_frames[:, 0:bins],
@@ -189,8 +209,13 @@ def tile_gmpahead_pa_e_kernel(tc, pooled, p, Wout_words, Wout_scales, out):
                 in1=p_sb[:, 0:bins, FRAMES // 2 : FRAMES, :],
                 op=MAX,
             )
-            leaky = work.tile([P, UNIT_BINS, C], F32)
-            nc.vector.tensor_tensor(out=leaky[:, 0:bins], in0=y[:, 0:bins], in1=sloped[:, 0:bins], op=MAX)
+            two_frames_of[u] = two_frames
+
+        def take_top_frame(u):
+            if u >= N_UNITS:
+                return
+            bins = bins_of(u)[1]
+            two_frames = two_frames_of[u]
             top_frame = work.tile([P, UNIT_BINS, C], BF16)
             nc.vector.tensor_tensor(
                 out=top_frame[:, 0:bins],
@@ -198,9 +223,25 @@ def tile_gmpahead_pa_e_kernel(tc, pooled, p, Wout_words, Wout_scales, out):
                 in1=two_frames[:, 0:bins, 1, :],
                 op=MAX,
             )
+            top_frame_of[u] = top_frame
+
+        def apply_leaky(u):
+            if u < 0:
+                return
+            bins = bins_of(u)[1]
+            leaky = work.tile([P, UNIT_BINS, C], F32)
+            nc.vector.tensor_tensor(
+                out=leaky[:, 0:bins], in0=y_of[u][:, 0:bins], in1=sloped_of[u][:, 0:bins], op=MAX
+            )
+            leaky_of[u] = leaky
+
+        def add_frame(u):
+            if u < 0:
+                return
+            bins = bins_of(u)[1]
             feat = results.tile([P, UNIT_BINS, C], F32)
             nc.vector.tensor_tensor(
-                out=feat[:, 0:bins], in0=leaky[:, 0:bins], in1=top_frame[:, 0:bins], op=ADD
+                out=feat[:, 0:bins], in0=leaky_of[u][:, 0:bins], in1=top_frame_of[u][:, 0:bins], op=ADD
             )
             feat_of[u] = feat
 
@@ -220,12 +261,21 @@ def tile_gmpahead_pa_e_kernel(tc, pooled, p, Wout_words, Wout_scales, out):
                 load_weights_and_frames(u)
             order_words(0)
             order_words(1)
-            transpose_and_quantise(0)
-            for u in range(N_UNITS):
+            order_words(2)
+            transpose_words(0)
+            transpose_words(1)
+            quantise(0)
+            for u in range(N_UNITS + 1):
                 load_pooled(u + LOAD_AHEAD + 2)
                 load_weights_and_frames(u + LOAD_AHEAD)
-                order_words(u + 2)
-                transpose_and_quantise(u + 1)
-                multiply_and_finish(u)
+                order_words(u + 3)
+                transpose_words(u + 2)
+                quantise(u + 1)
+                if u < N_UNITS:
+                    multiply(u)
+                halve_frames(u)
+                apply_leaky(u - 1)
+                take_top_frame(u)
+                add_frame(u - 1)
             for u in range(N_UNITS):
                 store(u)

@@ -33,6 +33,7 @@ SCALE_ROWS = 16
 QUADRANT = 32
 ROWS_PER_QUADRANT = SCALE_ROWS * QUADRANT // P
 PLANE_SET = 16
+PLANE_STEP = ROWS_PER_QUADRANT
 N_PLANE_SETS = (N_GROUPS + PLANE_SET - 1) // PLANE_SET
 
 LOAD_AHEAD = 7
@@ -80,17 +81,19 @@ def tile_gmpahead_pa_e_kernel(tc, pooled, p, Wout_words, Wout_scales, out):
             first = u * UNIT_BINS
             return first, min(UNIT_BINS, N_BINS - first)
 
-        def load_scale_planes(s):
+        def plane_start(u):
+            return PLANE_STEP * (u * UNIT_BINS * PASSES // PLANE_SET)
+
+        def load_scale_rows(s, r):
             first = s * PLANE_SET
             count = min(PLANE_SET, N_GROUPS - first)
             rows = Wout_scales[first : first + count].rearrange(
                 "g (q r) c -> r q g c", r=ROWS_PER_QUADRANT
             )
-            for r in range(ROWS_PER_QUADRANT):
-                nc.sync.dma_start(
-                    out=plane_sets[s][r:P:QUADRANT, 0:count, :].bitcast(I32),
-                    in_=rows[r].bitcast(I32),
-                )
+            nc.sync.dma_start(
+                out=plane_sets[s][PLANE_STEP * s + r : P : QUADRANT, 0:count, :].bitcast(I32),
+                in_=rows[r].bitcast(I32),
+            )
 
         def load_pooled(u):
             if u >= N_UNITS:
@@ -170,7 +173,7 @@ def tile_gmpahead_pa_e_kernel(tc, pooled, p, Wout_words, Wout_scales, out):
             code_scales = work.tile([P, UNIT_BINS * PASSES * B], U8, align_bytes=64)
             nc.vector.quantize_mx(
                 out=codes[:, 0:columns].bitcast(FP8X4),
-                scales=code_scales[:, 0:columns],
+                scales=code_scales[plane_start(u) : P, 0:columns],
                 in_=grouped[:, 0 : columns * PACK],
             )
             codes_of[u] = codes
@@ -186,9 +189,9 @@ def tile_gmpahead_pa_e_kernel(tc, pooled, p, Wout_words, Wout_scales, out):
                     nc.tensor.matmul_mx(
                         out=y[:, i, :],
                         lhsT=codes_of[u][:, b_cols].bitcast(FP8X4),
-                        lhsT_scale=code_scales_of[u][:, b_cols],
+                        lhsT_scale=code_scales_of[u][plane_start(u) : P, b_cols],
                         rhs=weights_of[u][:, i * PASSES + g, :].bitcast(FP8X4),
-                        rhs_scale=plane_sets[group // PLANE_SET][:, group % PLANE_SET, :],
+                        rhs_scale=plane_sets[group // PLANE_SET][plane_start(u) : P, group % PLANE_SET, :],
                         start=(g == 0),
                         stop=(g == PASSES - 1),
                     )
@@ -253,9 +256,10 @@ def tile_gmpahead_pa_e_kernel(tc, pooled, p, Wout_words, Wout_scales, out):
 
         with tc.manual_schedule():
             load_pooled(0)
-            for s in range(N_PLANE_SETS):
-                load_scale_planes(s)
             load_pooled(1)
+            for r in range(ROWS_PER_QUADRANT):
+                for s in range(N_PLANE_SETS):
+                    load_scale_rows(s, r)
             for u in range(LOAD_AHEAD):
                 load_pooled(u + 2)
                 load_weights_and_frames(u)

from contextlib import ExitStack

import concourse.mybir as mybir
from concourse.masks import make_identity

BF16 = mybir.dt.bfloat16
F32 = mybir.dt.float32
I32 = mybir.dt.int32
U32 = mybir.dt.uint32
U8 = mybir.dt.uint8
FP8X4 = mybir.dt.float8_e4m3fn_x4
MAX = mybir.AluOpType.max
ADD = mybir.AluOpType.add

P = 128
N_BINS = 31
B = 128
FRAMES = 4
C = 256
K = 1024
LEAKY_SLOPE = 0.01

PACK = 4
K_PASS = P * PACK
PASSES = K // K_PASS
PAIRS = PACK // 2
N_GROUPS = N_BINS * PASSES

UNIT_BINS = 2
N_UNITS = (N_BINS + UNIT_BINS - 1) // UNIT_BINS

SCALE_ROWS = 16
QUADRANT = 32
ROWS_PER_QUADRANT = SCALE_ROWS * QUADRANT // P
PLANE_SET = 16
PLANE_STEP = ROWS_PER_QUADRANT
N_PLANE_SETS = (N_GROUPS + PLANE_SET - 1) // PLANE_SET

LOAD_AHEAD = 7
LOAD_BUFS = LOAD_AHEAD + 3

FLOPS = 2 * N_BINS * B * K * C


def tile_gmpahead_pa_e_kernel(tc, pooled, p, Wout_words, Wout_scales, out):
    nc = tc.nc

    with ExitStack() as ctx:
        const = ctx.enter_context(tc.tile_pool(name="const", bufs=1))
        loads = ctx.enter_context(tc.tile_pool(name="loads", bufs=LOAD_BUFS))
        work = ctx.enter_context(tc.tile_pool(name="work", bufs=3))
        ordered_pool = ctx.enter_context(tc.tile_pool(name="ordered", bufs=3))
        results = ctx.enter_context(tc.tile_pool(name="results", bufs=N_UNITS))
        psum_t = ctx.enter_context(tc.psum_pool(name="psum_t", bufs=2 * PASSES))
        psum_y = ctx.enter_context(tc.psum_pool(name="psum_y", bufs=4))

        plane_sets = []
        for s in range(N_PLANE_SETS):
            planes = const.tile([P, PLANE_SET, C], U8, align_bytes=64, name="planes%d" % s)
            nc.vector.memset(planes[:].rearrange("p s c -> p (s c)").bitcast(I32), 0)
            plane_sets.append(planes)

        identity = const.tile([P, P], F32)
        make_identity(nc, identity[:])

        pooled_of = {}
        ordered_of = {}
        grouped_of = {}
        y_of = {}
        sloped_of = {}
        two_frames_of = {}
        top_frame_of = {}
        leaky_of = {}
        weights_of = {}
        frames_of = {}
        codes_of = {}
        code_scales_of = {}
        feat_of = {}

        def bins_of(u):
            first = u * UNIT_BINS
            return first, min(UNIT_BINS, N_BINS - first)

        def plane_start(u):
            return PLANE_STEP * (u * UNIT_BINS * PASSES // PLANE_SET)

        def load_scale_rows(s, r):
            first = s * PLANE_SET
            count = min(PLANE_SET, N_GROUPS - first)
            rows = Wout_scales[first : first + count].rearrange(
                "g (q r) c -> r q g c", r=ROWS_PER_QUADRANT
            )
            nc.sync.dma_start(
                out=plane_sets[s][PLANE_STEP * s + r : P : QUADRANT, 0:count, :].bitcast(I32),
                in_=rows[r].bitcast(I32),
            )

        def load_pooled(u):
            if u >= N_UNITS:
                return
            first, bins = bins_of(u)
            pooled_sb = loads.tile([P, UNIT_BINS * K], BF16)
            nc.sync.dma_start(
                out=pooled_sb[:, 0 : bins * K],
                in_=pooled[first : first + bins].rearrange("n (h s) k -> (n h) (s k)", s=bins),
            )
            pooled_of[u] = pooled_sb

        def load_weights_and_frames(u):
            if u >= N_UNITS:
                return
            first, bins = bins_of(u)
            groups = bins * PASSES
            w_sb = loads.tile([P, UNIT_BINS * PASSES, C], U32, align_bytes=64)
            nc.sync.dma_start(
                out=w_sb[:, 0:groups, :].bitcast(I32),
                in_=Wout_words[first * PASSES : first * PASSES + groups]
                .rearrange("g r c t -> r g (c t)")
                .bitcast(I32),
            )
            weights_of[u] = w_sb
            p_sb = loads.tile([P, UNIT_BINS, FRAMES, C], BF16)
            nc.sync.dma_start(
                out=p_sb[:, 0:bins],
                in_=p[first : first + bins].rearrange("n b t c -> b n t c"),
            )
            frames_of[u] = p_sb

        def order_words(u):
            if u >= N_UNITS:
                return
            bins = bins_of(u)[1]
            row_passes = bins * PASSES
            ordered = ordered_pool.tile([P, UNIT_BINS * K // 2], F32)
            nc.scalar.copy(
                out=ordered[:, 0 : bins * K // 2].rearrange("p (a w r) -> p a w r", a=row_passes, w=PAIRS),
                in_=pooled_of[u][:, 0 : bins * K]
                .bitcast(F32)
                .rearrange("p (a r w) -> p a w r", a=row_passes, w=PAIRS),
            )
            ordered_of[u] = ordered

        def transpose_words(u):
            if u >= N_UNITS:
                return
            bins = bins_of(u)[1]
            words = ordered_of[u]
            columns = bins * PASSES * B
            grouped = work.tile([P, UNIT_BINS * PASSES * B * PACK], BF16, align_bytes=64)
            grouped_words = (
                grouped[:, 0 : columns * PACK]
                .bitcast(F32)
                .rearrange("r (n g h su) -> r g n h su", n=bins, g=PASSES, su=bins * PAIRS)
            )
            for g in range(PASSES):
                xt = psum_t.tile([P, UNIT_BINS * PAIRS, B], F32)
                for s in range(bins):
                    for u2 in range(PAIRS):
                        begin = ((s * PASSES + g) * PAIRS + u2) * P
                        nc.tensor.transpose(xt[:, s * PAIRS + u2, :], words[:, begin : begin + P], identity[:])
                nc.scalar.copy(
                    out=grouped_words[:, g],
                    in_=xt[:, 0 : bins * PAIRS, :].rearrange("r su (n h) -> r n h su", n=bins),
                )
            grouped_of[u] = grouped

        def quantise(u):
            if u >= N_UNITS:
                return
            columns = bins_of(u)[1] * PASSES * B
            grouped = grouped_of[u]
            codes = work.tile([P, UNIT_BINS * PASSES * B], U32, align_bytes=64)
            code_scales = work.tile([P, UNIT_BINS * PASSES * B], U8, align_bytes=64)
            nc.vector.quantize_mx(
                out=codes[:, 0:columns].bitcast(FP8X4),
                scales=code_scales[plane_start(u) : P, 0:columns],
                in_=grouped[:, 0 : columns * PACK],
            )
            codes_of[u] = codes
            code_scales_of[u] = code_scales

        def multiply(u):
            first, bins = bins_of(u)
            y = psum_y.tile([P, UNIT_BINS, C], F32)
            for i in range(bins):
                for g in range(PASSES):
                    group = (first + i) * PASSES + g
                    b_cols = slice((i * PASSES + g) * B, (i * PASSES + g + 1) * B)
                    nc.tensor.matmul_mx(
                        out=y[:, i, :],
                        lhsT=codes_of[u][:, b_cols].bitcast(FP8X4),
                        lhsT_scale=code_scales_of[u][plane_start(u) : P, b_cols],
                        rhs=weights_of[u][:, i * PASSES + g, :].bitcast(FP8X4),
                        rhs_scale=plane_sets[group // PLANE_SET][plane_start(u) : P, group % PLANE_SET, :],
                        start=(g == 0),
                        stop=(g == PASSES - 1),
                    )
            sloped = work.tile([P, UNIT_BINS, C], F32)
            nc.scalar.mul(out=sloped[:, 0:bins], in_=y[:, 0:bins], mul=LEAKY_SLOPE)
            y_of[u] = y
            sloped_of[u] = sloped

        def halve_frames(u):
            if u >= N_UNITS:
                return
            bins = bins_of(u)[1]
            p_sb = frames_of[u]
            two_frames = work.tile([P, UNIT_BINS, FRAMES // 2, C], BF16)
            nc.vector.tensor_tensor(
                out=two_frames[:, 0:bins],
                in0=p_sb[:, 0:bins, 0 : FRAMES // 2, :],
                in1=p_sb[:, 0:bins, FRAMES // 2 : FRAMES, :],
                op=MAX,
            )
            two_frames_of[u] = two_frames

        def take_top_frame(u):
            if u >= N_UNITS:
                return
            bins = bins_of(u)[1]
            two_frames = two_frames_of[u]
            top_frame = work.tile([P, UNIT_BINS, C], BF16)
            nc.vector.tensor_tensor(
                out=top_frame[:, 0:bins],
                in0=two_frames[:, 0:bins, 0, :],
                in1=two_frames[:, 0:bins, 1, :],
                op=MAX,
            )
            top_frame_of[u] = top_frame

        def apply_leaky(u):
            if u < 0:
                return
            bins = bins_of(u)[1]
            leaky = work.tile([P, UNIT_BINS, C], F32)
            nc.vector.tensor_tensor(
                out=leaky[:, 0:bins], in0=y_of[u][:, 0:bins], in1=sloped_of[u][:, 0:bins], op=MAX
            )
            leaky_of[u] = leaky

        def add_frame(u):
            if u < 0:
                return
            bins = bins_of(u)[1]
            feat = results.tile([P, UNIT_BINS, C], F32)
            nc.vector.tensor_tensor(
                out=feat[:, 0:bins], in0=leaky_of[u][:, 0:bins], in1=top_frame_of[u][:, 0:bins], op=ADD
            )
            feat_of[u] = feat

        def store(u):
            first, bins = bins_of(u)
            nc.sync.dma_start(
                out=out[first : first + bins].rearrange("n b c -> b n c"), in_=feat_of[u][:, 0:bins]
            )

        with tc.manual_schedule():
            load_pooled(0)
            load_pooled(1)
            for r in range(ROWS_PER_QUADRANT):
                for s in range(N_PLANE_SETS):
                    load_scale_rows(s, r)
            for u in range(LOAD_AHEAD):
                load_pooled(u + 2)
                load_weights_and_frames(u)
            order_words(0)
            order_words(1)
            order_words(2)
            transpose_words(0)
            transpose_words(1)
            quantise(0)
            for u in range(N_UNITS + 1):
                load_pooled(u + LOAD_AHEAD + 2)
                load_weights_and_frames(u + LOAD_AHEAD)
                order_words(u + 3)
                transpose_words(u + 2)
                quantise(u + 1)
                if u < N_UNITS:
                    multiply(u)
                halve_frames(u)
                apply_leaky(u - 1)
                take_top_frame(u)
                add_frame(u - 1)
            for u in range(N_UNITS):
                store(u)
